import numpy as np
import ml_dtypes


def mxq(x, axis, fmt="e4m3"):
    dtype, down = {"e4m3": (ml_dtypes.float8_e4m3fn, 7), "e5m2": (ml_dtypes.float8_e5m2, 14)}[fmt]
    v = np.moveaxis(np.asarray(x, np.float32).astype(ml_dtypes.bfloat16).astype(np.float64), axis, -1)
    blocks = v.reshape(v.shape[:-1] + (-1, 32))
    amax = np.abs(blocks).max(-1, keepdims=True)
    byte = np.maximum(np.where(amax > 0, np.frexp(amax)[1] - 1 + 127, 0) - down, 1)
    scale = np.exp2(byte - 127.0)
    codes = (blocks / scale).astype(np.float32).astype(dtype).astype(np.float64)
    return np.moveaxis((codes * scale).reshape(v.shape), -1, axis)


WIDE = False


def mx_kscale(k):
    if not WIDE:
        return np.ones(k)
    levels = np.array([10, -10, 5, -5, 0])
    a = np.random.permutation(np.resize(levels, k // 512 * 4)).reshape(k // 512, 4)
    idx = np.arange(k)
    return np.exp2(a[idx // 512, idx % 128 // 32])


BF16 = ml_dtypes.bfloat16


def bf(x):
    return np.asarray(x, np.float32).astype(BF16)


def f64(x):
    return np.asarray(x).astype(np.float64)


B, L, D = 1, 1024, 512


def softmax(v):
    e = np.exp(v - v.max(-1, keepdims=True))
    return e / e.sum(-1, keepdims=True)


def setup_inputs():
    s, t = mx_kscale(D), mx_kscale(L)
    r = np.minimum(s, 1.0 / s)
    return {"Q": bf(np.random.standard_normal((B, L, D)) * s),
            "K": bf(np.random.standard_normal((B, L, D)) / s),
            "V": bf(np.random.standard_normal((B, L, D)) * np.sqrt(L) / 8.0 / t[:, None]),
            "adj_mask_matrix": bf((np.random.random((B, L, L)) < 0.5) * t),
            "com_mask_matrix": bf((np.random.random((B, L, L)) < 0.5) * t),
            "adj_rel": bf(np.random.standard_normal((1, 1, D)) * 0.5 * r),
            "com_rel": bf(np.random.standard_normal((1, 1, D)) * 0.5 * r),
            "scale": float(1.0 / np.sqrt(D))}


def reference(Q, K, V, adj_mask_matrix, com_mask_matrix, adj_rel, com_rel, scale):
    adj_Q = f64(Q) + f64(adj_rel)
    adj_K = f64(K) + f64(adj_rel)
    com_Q = f64(Q) + f64(com_rel)
    com_K = f64(K) + f64(com_rel)
    att_adj = (mxq(adj_Q, 2, "e4m3") @ mxq(adj_K, 2, "e4m3").transpose(0, 2, 1)) * scale
    att_com = (mxq(com_Q, 2, "e4m3") @ mxq(com_K, 2, "e4m3").transpose(0, 2, 1)) * scale
    mask_att = (softmax(att_adj) * f64(adj_mask_matrix)
                + softmax(att_com) * f64(com_mask_matrix))
    return mxq(mask_att, 2, "e4m3") @ mxq(f64(V), 1, "e4m3")

@@ -1,0 +1,322 @@
+from contextlib import ExitStack
+
+import concourse.mybir as mybir
+from concourse.masks import make_identity
+
+FLOPS = 3 * 2 * 1024 * 1024 * 512
+
+F32 = mybir.dt.float32
+BF16 = mybir.dt.bfloat16
+U32 = mybir.dt.uint32
+U8 = mybir.dt.uint8
+FP8X4 = mybir.dt.float8_e4m3fn_x4
+ALU = mybir.AluOpType
+ACT = mybir.ActivationFunctionType
+AX = mybir.AxisListType
+
+P = 128
+L = 1024
+D = 512
+NT = L // P
+MANUAL = True
+
+
+def tile_scaled_dot_product_attention_kernel(
+    tc, Q, K, V, adj_mask_matrix, com_mask_matrix, adj_rel, com_rel, scale, out
+):
+    nc = tc.nc
+    q2 = Q.flatten_outer_dims()
+    k2 = K.flatten_outer_dims()
+    v2 = V.flatten_outer_dims()
+    m2 = [adj_mask_matrix.flatten_outer_dims(), com_mask_matrix.flatten_outer_dims()]
+    rel_in = [adj_rel, com_rel]
+    out2 = out.flatten_outer_dims()
+
+    with ExitStack() as ctx:
+        keep = ctx.enter_context(tc.tile_pool(name="keep", bufs=1))
+        work = ctx.enter_context(tc.tile_pool(name="work", bufs=2))
+        small = ctx.enter_context(tc.tile_pool(name="small", bufs=4))
+        psum = ctx.enter_context(tc.psum_pool(name="psum", bufs=1))
+        if MANUAL:
+            ctx.enter_context(tc.manual_schedule())
+
+        def bank(b, name):
+            return psum.tile([P, 512], F32, tag="bank%d" % b, name=name)
+
+        ident = keep.tile([P, P], F32, name="ident")
+        make_identity(nc, ident[:])
+
+        warm = keep.tile([P, 1], F32, name="warm")
+        nc.vector.memset(warm[:], 0.0)
+        nc.scalar.activation(out=warm[:], in_=warm[:], func=ACT.Exp)
+
+        rel = [keep.tile([P, 4], BF16, name="rel%d" % w) for w in range(2)]
+        with nc.allow_non_contiguous_dma(reason="512 values, two pairs to a partition"):
+            for w in range(2):
+                nc.sync.dma_start(
+                    out=rel[w][:].rearrange("p (u e) -> p u e", u=2),
+                    in_=rel_in[w][0, 0, :].rearrange("(u p e) -> p u e", u=2, p=P, e=2),
+                )
+
+        k_sb = keep.tile([P, NT * D], BF16, name="k_sb")
+        q_sb = keep.tile([P, NT * D], BF16, name="q_sb")
+        v_sb = keep.tile([P, NT * D], BF16, name="v_sb")
+        m_sb = [keep.tile([P, NT * L], BF16, name="m_sb%d" % w) for w in range(2)]
+
+        def load_rows(dst, src, first, count):
+            nc.sync.dma_start(
+                out=dst[:, first * D : (first + count) * D].rearrange("p (n d) -> p n d", n=count),
+                in_=src[first * P : (first + count) * P, :].rearrange("(n p) d -> p n d", p=P),
+            )
+
+        for c in range(4):
+            load_rows(k_sb, k2, 2 * c, 2)
+        load_rows(q_sb, q2, 0, 2)
+        load_rows(v_sb, v2, 0, 4)
+        load_rows(v_sb, v2, 4, 4)
+        for c in range(1, 4):
+            load_rows(q_sb, q2, 2 * c, 2)
+        for i in range(NT):
+            for w in range(2):
+                nc.sync.dma_start(
+                    out=m_sb[w][:, i * L : (i + 1) * L], in_=m2[w][i * P : (i + 1) * P, :]
+                )
+
+        kc = [keep.tile([P, L], U32, name="kc%d" % w, align_bytes=64) for w in range(2)]
+        ks = [keep.tile([P, L], U8, name="ks%d" % w, align_bytes=64) for w in range(2)]
+        qc = keep.tile([P, 4 * 512], U32, name="qc", align_bytes=64)
+        qs = keep.tile([P, 4 * 512], U8, name="qs", align_bytes=64)
+        vc = keep.tile([P, 2 * D], U32, name="vc", align_bytes=64)
+        vs = keep.tile([P, 2 * D], U8, name="vs", align_bytes=64)
+        gv = keep.tile([P, 2 * 4 * D], BF16, name="gv", align_bytes=64)
+        gk = [
+            [keep.tile([P, 2048], BF16, name="gk%d%d" % (w, h), align_bytes=64) for h in range(2)]
+            for w in range(2)
+        ]
+
+        k_w = k_sb[:].bitcast(F32)
+        q_w = q_sb[:].bitcast(F32)
+
+        def transposes(src_w, c, b, name):
+            xt = bank(b, name)
+            xv = xt[:].rearrange("p (n r u) -> p n r u", n=2, r=P, u=2)
+            for n in range(2):
+                for u in range(2):
+                    col = (2 * c + n) * 256 + u * P
+                    nc.tensor.transpose(xv[:, n, :, u], src_w[:, col : col + P], ident[:])
+            return xt
+
+        def add_rel(dst, xt, w):
+            nc.vector.tensor_tensor(
+                out=dst.rearrange("p (x t) -> p x t", t=4),
+                in0=xt[:].bitcast(BF16).rearrange("p (x t) -> p x t", t=4),
+                in1=rel[w][:].unsqueeze(1).to_broadcast([P, 256, 4]),
+                op=ALU.add,
+            )
+
+        def quant(codes, scales, src):
+            nc.vector.quantize_mx(out=codes.bitcast(FP8X4), scales=scales, in_=src)
+
+        def quant_k(w, h):
+            quant(kc[w][:, h * 512 : (h + 1) * 512], ks[w][:, h * 512 : (h + 1) * 512], gk[w][h][:])
+
+        xk = [transposes(k_w, c, c, "xk%d" % c) for c in range(4)]
+        xq = [transposes(q_w, c, 4 + c, "xq%d" % c) for c in range(4)]
+
+        for g in range(2):
+            nc.scalar.copy(
+                out=gv[:, g * 2048 : (g + 1) * 2048].rearrange("p (c i t) -> p c t i", i=4, t=4),
+                in_=v_sb[:, g * 2048 : (g + 1) * 2048].rearrange("p (t c i) -> p c t i", t=4, i=4),
+            )
+
+        def quant_v(g):
+            quant(vc[:, g * D : (g + 1) * D], vs[:, g * D : (g + 1) * D], gv[:, g * 2048 : (g + 1) * 2048])
+
+        gq = {}
+
+        def q_adds(c):
+            gq[c] = work.tile([P, 2048], BF16, tag="gq", name="gq%d" % c, align_bytes=64)
+            for w in range(2):
+                add_rel(gq[c][:, w * 1024 : (w + 1) * 1024], xq[c], w)
+
+        def q_quant(c):
+            quant(qc[:, c * 512 : (c + 1) * 512], qs[:, c * 512 : (c + 1) * 512], gq[c][:])
+
+        for c in range(4):
+            for w in range(2):
+                add_rel(gk[w][c // 2][:, (c % 2) * 1024 : (c % 2 + 1) * 1024], xk[c], w)
+                if c == 2:
+                    quant_k(w, 0)
+        q_adds(0)
+        quant_k(0, 1)
+        quant_k(1, 1)
+        q_quant(0)
+
+        sc = {}
+        st = {}
+        e_t = {}
+        t_t = {}
+        pt = {}
+        gp = {}
+        pq = {}
+        o_ps = {}
+
+        def scores(i, w):
+            off = ((i // 2) * 2 + w) * 256 + (i % 2) * P
+            tiles = []
+            for h in range(2):
+                t = bank(2 * w + h, "sc%d_%d_%d" % (i, w, h))
+                nc.tensor.matmul_mx(
+                    out=t[:],
+                    lhsT=qc[:, off : off + P].bitcast(FP8X4),
+                    lhsT_scale=qs[:, off : off + P],
+                    rhs=kc[w][:, h * 512 : (h + 1) * 512].bitcast(FP8X4),
+                    rhs_scale=ks[w][:, h * 512 : (h + 1) * 512],
+                    start=True,
+                    stop=True,
+                )
+                tiles.append(t)
+            sc[(i, w)] = tiles
+
+        def row_max(i, w):
+            if w == 0:
+                st[i] = {
+                    "mx": small.tile([P, 4], F32, tag="mx", name="mx%d" % i),
+                    "nb": small.tile([P, 2], F32, tag="nb", name="nb%d" % i),
+                    "sm": small.tile([P, 4], F32, tag="sm", name="sm%d" % i),
+                    "tot": small.tile([P, 2], F32, tag="tot", name="tot%d" % i),
+                    "rc": small.tile([P, 2], F32, tag="rc", name="rc%d" % i),
+                }
+            mx = st[i]["mx"]
+            for h in range(2):
+                nc.vector.tensor_reduce(
+                    out=mx[:, 2 * w + h : 2 * w + h + 1], in_=sc[(i, w)][h][:], axis=AX.X, op=ALU.max
+                )
+            nc.vector.tensor_scalar(
+                out=st[i]["nb"][:, w : w + 1],
+                in0=mx[:, 2 * w : 2 * w + 1],
+                scalar1=mx[:, 2 * w + 1 : 2 * w + 2],
+                scalar2=-scale,
+                op0=ALU.max,
+                op1=ALU.mult,
+            )
+
+        def exps(i, w):
+            e = work.tile([P, L], F32, tag="e%d" % w, name="e%d_%d" % (i, w))
+            for h in range(2):
+                nc.scalar.activation(
+                    out=e[:, h * 512 : (h + 1) * 512],
+                    in_=sc[(i, w)][h][:],
+                    func=ACT.Exp,
+                    bias=st[i]["nb"][:, w : w + 1],
+                    scale=scale,
+                    accum_out=st[i]["sm"][:, 2 * w + h : 2 * w + h + 1],
+                )
+            e_t[(i, w)] = e
+
+        def recip(i):
+            nc.vector.tensor_reduce(
+                out=st[i]["tot"][:],
+                in_=st[i]["sm"][:].rearrange("p (w h) -> p w h", h=2),
+                axis=AX.X,
+                op=ALU.add,
+            )
+            nc.vector.reciprocal(out=st[i]["rc"][:], in_=st[i]["tot"][:])
+
+        def masked(i, w):
+            t = work.tile([P, L], F32, tag="t%d" % w, name="t%d_%d" % (i, w))
+            nc.vector.scalar_tensor_tensor(
+                out=t[:],
+                in0=e_t[(i, w)][:],
+                scalar=st[i]["rc"][:, w : w + 1],
+                in1=m_sb[w][:, i * L : (i + 1) * L],
+                op0=ALU.mult,
+                op1=ALU.mult,
+            )
+            t_t[(i, w)] = t
+
+        def flip(i):
+            tiles = []
+            for g in range(2):
+                x = bank(4 + g, "pt%d_%d" % (i, g))
+                for t in range(4):
+                    kb = 4 * g + t
+                    for w in range(2):
+                        nc.tensor.matmul(
+                            out=x[:, t * P : (t + 1) * P],
+                            lhsT=t_t[(i, w)][:, kb * P : (kb + 1) * P],
+                            rhs=ident[:],
+                            is_transpose=True,
+                            start=(w == 0),
+                            stop=(w == 1),
+                        )
+                tiles.append(x)
+            pt[i] = tiles
+
+        def round_p(i):
+            x = work.tile([P, L], BF16, tag="gp", name="gp%d" % i, align_bytes=64)
+            for g in range(2):
+                nc.scalar.copy(
+                    out=x[:, g * 512 : (g + 1) * 512].rearrange("p (r t) -> p r t", t=4),
+                    in_=pt[i][g][:].rearrange("p (t r) -> p r t", t=4),
+                )
+            gp[i] = x
+
+        def quant_p(i):
+            codes = work.tile([P, 256], U32, tag="pc", name="pc%d" % i, align_bytes=64)
+            scales = work.tile([P, 256], U8, tag="ps", name="ps%d" % i, align_bytes=64)
+            quant(codes[:], scales[:], gp[i][:])
+            pq[i] = (codes, scales)
+
+        def pv(i):
+            codes, scales = pq[i]
+            o = bank(6 + i % 2, "o%d" % i)
+            for g in range(2):
+                nc.tensor.matmul_mx(
+                    out=o[:],
+                    lhsT=codes[:, g * P : (g + 1) * P].bitcast(FP8X4),
+                    lhsT_scale=scales[:, g * P : (g + 1) * P],
+                    rhs=vc[:, g * D : (g + 1) * D].bitcast(FP8X4),
+                    rhs_scale=vs[:, g * D : (g + 1) * D],
+                    start=(g == 0),
+                    stop=(g == 1),
+                )
+            o_ps[i] = o
+
+        def store(i):
+            o = work.tile([P, D], F32, tag="o_sb", name="o_sb%d" % i, bufs=3)
+            nc.scalar.copy(out=o[:], in_=o_ps[i][:])
+            nc.sync.dma_start(out=out2[i * P : (i + 1) * P, :], in_=o[:])
+
+        scores(0, 0)
+        scores(0, 1)
+        for j in range(NT + 3):
+            for w in range(2):
+                if j < NT:
+                    row_max(j, w)
+                    exps(j, w)
+                if j + 1 < NT:
+                    scores(j + 1, w)
+            if j in (1, 2):
+                q_adds(j + 1)
+            if 0 <= j - 1 < NT:
+                recip(j - 1)
+                masked(j - 1, 0)
+            if 0 <= j - 3 < NT:
+                quant_p(j - 3)
+                pv(j - 3)
+            if 0 <= j - 1 < NT:
+                masked(j - 1, 1)
+            if 0 <= j - 2 < NT:
+                round_p(j - 2)
+            if 0 <= j - 1 < NT:
+                flip(j - 1)
+            if 0 <= j - 3 < NT:
+                store(j - 3)
+            if j == 0:
+                q_adds(1)
+                quant_v(0)
+                q_quant(1)
+                quant_v(1)
+            if j in (1, 2):
+                q_quant(j + 1)

@@ -18,7 +18,6 @@ P = 128
 L = 1024
 D = 512
 NT = L // P
-MANUAL = True
 
 
 def tile_scaled_dot_product_attention_kernel(
@@ -37,8 +36,7 @@ def tile_scaled_dot_product_attention_kernel(
         work = ctx.enter_context(tc.tile_pool(name="work", bufs=2))
         small = ctx.enter_context(tc.tile_pool(name="small", bufs=4))
         psum = ctx.enter_context(tc.psum_pool(name="psum", bufs=1))
-        if MANUAL:
-            ctx.enter_context(tc.manual_schedule())
+        ctx.enter_context(tc.manual_schedule())
 
         def bank(b, name):
             return psum.tile([P, 512], F32, tag="bank%d" % b, name=name)
@@ -46,17 +44,17 @@ def tile_scaled_dot_product_attention_kernel(
         ident = keep.tile([P, P], F32, name="ident")
         make_identity(nc, ident[:])
 
-        warm = keep.tile([P, 1], F32, name="warm")
-        nc.vector.memset(warm[:], 0.0)
-        nc.scalar.activation(out=warm[:], in_=warm[:], func=ACT.Exp)
-
         rel = [keep.tile([P, 4], BF16, name="rel%d" % w) for w in range(2)]
         with nc.allow_non_contiguous_dma(reason="512 values, two pairs to a partition"):
             for w in range(2):
-                nc.sync.dma_start(
+                nc.scalar.dma_start(
                     out=rel[w][:].rearrange("p (u e) -> p u e", u=2),
                     in_=rel_in[w][0, 0, :].rearrange("(u p e) -> p u e", u=2, p=P, e=2),
                 )
+
+        warm = keep.tile([P, 1], F32, name="warm")
+        nc.vector.memset(warm[:], 0.0)
+        nc.scalar.activation(out=warm[:], in_=warm[:], func=ACT.Exp)
 
         k_sb = keep.tile([P, NT * D], BF16, name="k_sb")
         q_sb = keep.tile([P, NT * D], BF16, name="q_sb")
@@ -142,16 +140,6 @@ def tile_scaled_dot_product_attention_kernel(
         def q_quant(c):
             quant(qc[:, c * 512 : (c + 1) * 512], qs[:, c * 512 : (c + 1) * 512], gq[c][:])
 
-        for c in range(4):
-            for w in range(2):
-                add_rel(gk[w][c // 2][:, (c % 2) * 1024 : (c % 2 + 1) * 1024], xk[c], w)
-                if c == 2:
-                    quant_k(w, 0)
-        q_adds(0)
-        quant_k(0, 1)
-        quant_k(1, 1)
-        q_quant(0)
-
         sc = {}
         st = {}
         e_t = {}
@@ -178,8 +166,8 @@ def tile_scaled_dot_product_attention_kernel(
                 tiles.append(t)
             sc[(i, w)] = tiles
 
-        def row_max(i, w):
-            if w == 0:
+        def red(i, w, h):
+            if (w, h) == (0, 0):
                 st[i] = {
                     "mx": small.tile([P, 4], F32, tag="mx", name="mx%d" % i),
                     "nb": small.tile([P, 2], F32, tag="nb", name="nb%d" % i),
@@ -187,11 +175,12 @@ def tile_scaled_dot_product_attention_kernel(
                     "tot": small.tile([P, 2], F32, tag="tot", name="tot%d" % i),
                     "rc": small.tile([P, 2], F32, tag="rc", name="rc%d" % i),
                 }
+            nc.vector.tensor_reduce(
+                out=st[i]["mx"][:, 2 * w + h : 2 * w + h + 1], in_=sc[(i, w)][h][:], axis=AX.X, op=ALU.max
+            )
+
+        def nbias(i, w):
             mx = st[i]["mx"]
-            for h in range(2):
-                nc.vector.tensor_reduce(
-                    out=mx[:, 2 * w + h : 2 * w + h + 1], in_=sc[(i, w)][h][:], axis=AX.X, op=ALU.max
-                )
             nc.vector.tensor_scalar(
                 out=st[i]["nb"][:, w : w + 1],
                 in0=mx[:, 2 * w : 2 * w + 1],
@@ -214,109 +203,160 @@ def tile_scaled_dot_product_attention_kernel(
                 )
             e_t[(i, w)] = e
 
-        def recip(i):
+        def total(i):
             nc.vector.tensor_reduce(
                 out=st[i]["tot"][:],
                 in_=st[i]["sm"][:].rearrange("p (w h) -> p w h", h=2),
                 axis=AX.X,
                 op=ALU.add,
             )
+
+        def recip(i):
             nc.vector.reciprocal(out=st[i]["rc"][:], in_=st[i]["tot"][:])
 
-        def masked(i, w):
-            t = work.tile([P, L], F32, tag="t%d" % w, name="t%d_%d" % (i, w))
+        def masked(i, w, lo, hi):
+            if lo == 0:
+                t_t[(i, w)] = work.tile([P, L], F32, tag="t%d" % w, name="t%d_%d" % (i, w))
             nc.vector.scalar_tensor_tensor(
-                out=t[:],
-                in0=e_t[(i, w)][:],
+                out=t_t[(i, w)][:, lo * P : hi * P],
+                in0=e_t[(i, w)][:, lo * P : hi * P],
                 scalar=st[i]["rc"][:, w : w + 1],
-                in1=m_sb[w][:, i * L : (i + 1) * L],
+                in1=m_sb[w][:, i * L + lo * P : i * L + hi * P],
                 op0=ALU.mult,
                 op1=ALU.mult,
             )
-            t_t[(i, w)] = t
 
-        def flip(i):
-            tiles = []
-            for g in range(2):
-                x = bank(4 + g, "pt%d_%d" % (i, g))
-                for t in range(4):
-                    kb = 4 * g + t
-                    for w in range(2):
-                        nc.tensor.matmul(
-                            out=x[:, t * P : (t + 1) * P],
-                            lhsT=t_t[(i, w)][:, kb * P : (kb + 1) * P],
-                            rhs=ident[:],
-                            is_transpose=True,
-                            start=(w == 0),
-                            stop=(w == 1),
-                        )
-                tiles.append(x)
-            pt[i] = tiles
+        def flip(i, g):
+            x = bank(4 + g, "pt%d_%d" % (i, g))
+            for t in range(4):
+                kb = 4 * g + t
+                for w in range(2):
+                    nc.tensor.matmul(
+                        out=x[:, t * P : (t + 1) * P],
+                        lhsT=t_t[(i, w)][:, kb * P : (kb + 1) * P],
+                        rhs=ident[:],
+                        is_transpose=True,
+                        start=(w == 0),
+                        stop=(w == 1),
+                    )
+            pt[(i, g)] = x
 
-        def round_p(i):
-            x = work.tile([P, L], BF16, tag="gp", name="gp%d" % i, align_bytes=64)
-            for g in range(2):
-                nc.scalar.copy(
-                    out=x[:, g * 512 : (g + 1) * 512].rearrange("p (r t) -> p r t", t=4),
-                    in_=pt[i][g][:].rearrange("p (t r) -> p r t", t=4),
+        def round_p(i, g, on_vector=False):
+            if g == 0:
+                gp[i] = work.tile([P, L], BF16, tag="gp", name="gp%d" % i, align_bytes=64)
+            dst = gp[i][:, g * 512 : (g + 1) * 512].rearrange("p (r t) -> p r t", t=4)
+            src = pt[(i, g)][:].rearrange("p (t r) -> p r t", t=4)
+            if on_vector:
+                nc.vector.tensor_copy(out=dst, in_=src)
+            else:
+                nc.scalar.copy(out=dst, in_=src)
+
+        def quant_p(i, lo, hi):
+            if lo == 0:
+                pq[i] = (
+                    work.tile([P, 256], U32, tag="pc", name="pc%d" % i, align_bytes=64),
+                    work.tile([P, 256], U8, tag="ps", name="ps%d" % i, align_bytes=64),
                 )
-            gp[i] = x
-
-        def quant_p(i):
-            codes = work.tile([P, 256], U32, tag="pc", name="pc%d" % i, align_bytes=64)
-            scales = work.tile([P, 256], U8, tag="ps", name="ps%d" % i, align_bytes=64)
-            quant(codes[:], scales[:], gp[i][:])
-            pq[i] = (codes, scales)
-
-        def pv(i):
             codes, scales = pq[i]
-            o = bank(6 + i % 2, "o%d" % i)
-            for g in range(2):
-                nc.tensor.matmul_mx(
-                    out=o[:],
-                    lhsT=codes[:, g * P : (g + 1) * P].bitcast(FP8X4),
-                    lhsT_scale=scales[:, g * P : (g + 1) * P],
-                    rhs=vc[:, g * D : (g + 1) * D].bitcast(FP8X4),
-                    rhs_scale=vs[:, g * D : (g + 1) * D],
-                    start=(g == 0),
-                    stop=(g == 1),
-                )
-            o_ps[i] = o
+            quant(codes[:, lo * P : hi * P], scales[:, lo * P : hi * P], gp[i][:, lo * 512 : hi * 512])
+
+        def pv(i, g):
+            codes, scales = pq[i]
+            if g == 0:
+                o_ps[i] = bank(6 + i % 2, "o%d" % i)
+            nc.tensor.matmul_mx(
+                out=o_ps[i][:],
+                lhsT=codes[:, g * P : (g + 1) * P].bitcast(FP8X4),
+                lhsT_scale=scales[:, g * P : (g + 1) * P],
+                rhs=vc[:, g * D : (g + 1) * D].bitcast(FP8X4),
+                rhs_scale=vs[:, g * D : (g + 1) * D],
+                start=(g == 0),
+                stop=(g == 1),
+            )
 
         def store(i):
             o = work.tile([P, D], F32, tag="o_sb", name="o_sb%d" % i, bufs=3)
             nc.scalar.copy(out=o[:], in_=o_ps[i][:])
             nc.sync.dma_start(out=out2[i * P : (i + 1) * P, :], in_=o[:])
 
+        for c in range(4):
+            for w in range(2):
+                add_rel(gk[w][c // 2][:, (c % 2) * 1024 : (c % 2 + 1) * 1024], xk[c], w)
+                if c == 2:
+                    quant_k(w, 0)
+        q_adds(0)
+        quant_k(0, 1)
+        quant_k(1, 1)
+        q_quant(0)
         scores(0, 0)
         scores(0, 1)
-        for j in range(NT + 3):
-            for w in range(2):
-                if j < NT:
-                    row_max(j, w)
-                    exps(j, w)
-                if j + 1 < NT:
-                    scores(j + 1, w)
+        q_adds(1)
+
+        for j in range(NT):
+            red(j, 0, 0)
+            if j >= 1:
+                total(j - 1)
+            red(j, 0, 1)
+            if j >= 1:
+                recip(j - 1)
+            red(j, 1, 0)
+            nbias(j, 0)
+            exps(j, 0)
+            if j + 1 < NT:
+                scores(j + 1, 0)
+            red(j, 1, 1)
+            if j == 0:
+                quant_v(0)
+            if j >= 3:
+                quant_p(j - 3, 0, 2)
+                pv(j - 3, 0)
+                pv(j - 3, 1)
+            nbias(j, 1)
+            exps(j, 1)
+            if j + 1 < NT:
+                scores(j + 1, 1)
             if j in (1, 2):
                 q_adds(j + 1)
-            if 0 <= j - 1 < NT:
-                recip(j - 1)
-                masked(j - 1, 0)
-            if 0 <= j - 3 < NT:
-                quant_p(j - 3)
-                pv(j - 3)
-            if 0 <= j - 1 < NT:
-                masked(j - 1, 1)
-            if 0 <= j - 2 < NT:
-                round_p(j - 2)
-            if 0 <= j - 1 < NT:
-                flip(j - 1)
-            if 0 <= j - 3 < NT:
+            if j >= 1:
+                masked(j - 1, 0, 0, 8)
+                masked(j - 1, 1, 0, 8)
+            if j >= 2:
+                round_p(j - 2, 0)
+                round_p(j - 2, 1)
+            if j >= 1:
+                flip(j - 1, 0)
+                flip(j - 1, 1)
+            if j >= 3:
                 store(j - 3)
             if j == 0:
-                q_adds(1)
-                quant_v(0)
                 q_quant(1)
                 quant_v(1)
             if j in (1, 2):
                 q_quant(j + 1)
+
+        z = NT - 1
+        total(z)
+        quant_p(z - 2, 0, 2)
+        pv(z - 2, 0)
+        pv(z - 2, 1)
+        recip(z)
+        round_p(z - 1, 0)
+        round_p(z - 1, 1)
+        masked(z, 0, 0, 4)
+        masked(z, 1, 0, 4)
+        flip(z, 0)
+        masked(z, 0, 4, 8)
+        masked(z, 1, 4, 8)
+        flip(z, 1)
+        store(z - 2)
+        quant_p(z - 1, 0, 2)
+        pv(z - 1, 0)
+        pv(z - 1, 1)
+        round_p(z, 0)
+        quant_p(z, 0, 1)
+        pv(z, 0)
+        round_p(z, 1, on_vector=True)
+        store(z - 1)
+        quant_p(z, 1, 2)
+        pv(z, 1)
+        store(z)

@@ -18,6 +18,7 @@ P = 128
 L = 1024
 D = 512
 NT = L // P
+VB = 4
 
 
 def tile_scaled_dot_product_attention_kernel(
@@ -214,9 +215,32 @@ def tile_scaled_dot_product_attention_kernel(
         def recip(i):
             nc.vector.reciprocal(out=st[i]["rc"][:], in_=st[i]["tot"][:])
 
+        def new_t(i, w):
+            t_t[(i, w)] = work.tile([P, L], F32, tag="t%d" % w, name="t%d_%d" % (i, w))
+
+        def pool_mul(i, lo, hi):
+            new_t(i, 1)
+            for b in range(lo, hi, 2):
+                nc.gpsimd.tensor_tensor(
+                    out=t_t[(i, 1)][:, b * P : (b + 2) * P],
+                    in0=e_t[(i, 1)][:, b * P : (b + 2) * P],
+                    in1=m_sb[1][:, i * L + b * P : i * L + (b + 2) * P],
+                    op=ALU.mult,
+                )
+
+        def pool_scale(i, lo, hi):
+            nc.gpsimd.tensor_scalar(
+                out=t_t[(i, 1)][:, lo * P : hi * P],
+                in0=t_t[(i, 1)][:, lo * P : hi * P],
+                scalar1=st[i]["rc"][:, 1:2],
+                scalar2=0.0,
+                op0=ALU.mult,
+                op1=ALU.add,
+            )
+
         def masked(i, w, lo, hi):
-            if lo == 0:
-                t_t[(i, w)] = work.tile([P, L], F32, tag="t%d" % w, name="t%d_%d" % (i, w))
+            if (i, w) not in t_t:
+                new_t(i, w)
             nc.vector.scalar_tensor_tensor(
                 out=t_t[(i, w)][:, lo * P : hi * P],
                 in0=e_t[(i, w)][:, lo * P : hi * P],
@@ -299,6 +323,7 @@ def tile_scaled_dot_product_attention_kernel(
             red(j, 0, 1)
             if j >= 1:
                 recip(j - 1)
+                pool_scale(j - 1, VB, 8)
             red(j, 1, 0)
             nbias(j, 0)
             exps(j, 0)
@@ -314,12 +339,13 @@ def tile_scaled_dot_product_attention_kernel(
             nbias(j, 1)
             exps(j, 1)
             if j + 1 < NT:
+                pool_mul(j, VB, 8)
                 scores(j + 1, 1)
             if j in (1, 2):
                 q_adds(j + 1)
             if j >= 1:
                 masked(j - 1, 0, 0, 8)
-                masked(j - 1, 1, 0, 8)
+                masked(j - 1, 1, 0, VB)
             if j >= 2:
                 round_p(j - 2, 0)
                 round_p(j - 2, 1)

from contextlib import ExitStack

import concourse.mybir as mybir
from concourse.masks import make_identity

FLOPS = 3 * 2 * 1024 * 1024 * 512

F32 = mybir.dt.float32
BF16 = mybir.dt.bfloat16
U32 = mybir.dt.uint32
U8 = mybir.dt.uint8
FP8X4 = mybir.dt.float8_e4m3fn_x4
ALU = mybir.AluOpType
ACT = mybir.ActivationFunctionType
AX = mybir.AxisListType

P = 128
L = 1024
D = 512
NT = L // P
VB = 4


def tile_scaled_dot_product_attention_kernel(
    tc, Q, K, V, adj_mask_matrix, com_mask_matrix, adj_rel, com_rel, scale, out
):
    nc = tc.nc
    q2 = Q.flatten_outer_dims()
    k2 = K.flatten_outer_dims()
    v2 = V.flatten_outer_dims()
    m2 = [adj_mask_matrix.flatten_outer_dims(), com_mask_matrix.flatten_outer_dims()]
    rel_in = [adj_rel, com_rel]
    out2 = out.flatten_outer_dims()

    with ExitStack() as ctx:
        keep = ctx.enter_context(tc.tile_pool(name="keep", bufs=1))
        work = ctx.enter_context(tc.tile_pool(name="work", bufs=2))
        small = ctx.enter_context(tc.tile_pool(name="small", bufs=4))
        psum = ctx.enter_context(tc.psum_pool(name="psum", bufs=1))
        ctx.enter_context(tc.manual_schedule())

        def bank(b, name):
            return psum.tile([P, 512], F32, tag="bank%d" % b, name=name)

        ident = keep.tile([P, P], F32, name="ident")
        make_identity(nc, ident[:])

        rel = [keep.tile([P, 4], BF16, name="rel%d" % w) for w in range(2)]
        with nc.allow_non_contiguous_dma(reason="512 values, two pairs to a partition"):
            for w in range(2):
                nc.scalar.dma_start(
                    out=rel[w][:].rearrange("p (u e) -> p u e", u=2),
                    in_=rel_in[w][0, 0, :].rearrange("(u p e) -> p u e", u=2, p=P, e=2),
                )

        warm = keep.tile([P, 1], F32, name="warm")
        nc.vector.memset(warm[:], 0.0)
        nc.scalar.activation(out=warm[:], in_=warm[:], func=ACT.Exp)

        k_sb = keep.tile([P, NT * D], BF16, name="k_sb")
        q_sb = keep.tile([P, NT * D], BF16, name="q_sb")
        v_sb = keep.tile([P, NT * D], BF16, name="v_sb")
        m_sb = [keep.tile([P, NT * L], BF16, name="m_sb%d" % w) for w in range(2)]

        def load_rows(dst, src, first, count):
            nc.sync.dma_start(
                out=dst[:, first * D : (first + count) * D].rearrange("p (n d) -> p n d", n=count),
                in_=src[first * P : (first + count) * P, :].rearrange("(n p) d -> p n d", p=P),
            )

        for c in range(4):
            load_rows(k_sb, k2, 2 * c, 2)
        load_rows(q_sb, q2, 0, 2)
        load_rows(v_sb, v2, 0, 4)
        load_rows(v_sb, v2, 4, 4)
        for c in range(1, 4):
            load_rows(q_sb, q2, 2 * c, 2)
        for i in range(NT):
            for w in range(2):
                nc.sync.dma_start(
                    out=m_sb[w][:, i * L : (i + 1) * L], in_=m2[w][i * P : (i + 1) * P, :]
                )

        kc = [keep.tile([P, L], U32, name="kc%d" % w, align_bytes=64) for w in range(2)]
        ks = [keep.tile([P, L], U8, name="ks%d" % w, align_bytes=64) for w in range(2)]
        qc = keep.tile([P, 4 * 512], U32, name="qc", align_bytes=64)
        qs = keep.tile([P, 4 * 512], U8, name="qs", align_bytes=64)
        vc = keep.tile([P, 2 * D], U32, name="vc", align_bytes=64)
        vs = keep.tile([P, 2 * D], U8, name="vs", align_bytes=64)
        gv = keep.tile([P, 2 * 4 * D], BF16, name="gv", align_bytes=64)
        gk = [
            [keep.tile([P, 2048], BF16, name="gk%d%d" % (w, h), align_bytes=64) for h in range(2)]
            for w in range(2)
        ]

        k_w = k_sb[:].bitcast(F32)
        q_w = q_sb[:].bitcast(F32)

        def transposes(src_w, c, b, name):
            xt = bank(b, name)
            xv = xt[:].rearrange("p (n r u) -> p n r u", n=2, r=P, u=2)
            for n in range(2):
                for u in range(2):
                    col = (2 * c + n) * 256 + u * P
                    nc.tensor.transpose(xv[:, n, :, u], src_w[:, col : col + P], ident[:])
            return xt

        def add_rel(dst, xt, w):
            nc.vector.tensor_tensor(
                out=dst.rearrange("p (x t) -> p x t", t=4),
                in0=xt[:].bitcast(BF16).rearrange("p (x t) -> p x t", t=4),
                in1=rel[w][:].unsqueeze(1).to_broadcast([P, 256, 4]),
                op=ALU.add,
            )

        def quant(codes, scales, src):
            nc.vector.quantize_mx(out=codes.bitcast(FP8X4), scales=scales, in_=src)

        def quant_k(w, h):
            quant(kc[w][:, h * 512 : (h + 1) * 512], ks[w][:, h * 512 : (h + 1) * 512], gk[w][h][:])

        xk = [transposes(k_w, c, c, "xk%d" % c) for c in range(4)]
        xq = [transposes(q_w, c, 4 + c, "xq%d" % c) for c in range(4)]

        for g in range(2):
            nc.scalar.copy(
                out=gv[:, g * 2048 : (g + 1) * 2048].rearrange("p (c i t) -> p c t i", i=4, t=4),
                in_=v_sb[:, g * 2048 : (g + 1) * 2048].rearrange("p (t c i) -> p c t i", t=4, i=4),
            )

        def quant_v(g):
            quant(vc[:, g * D : (g + 1) * D], vs[:, g * D : (g + 1) * D], gv[:, g * 2048 : (g + 1) * 2048])

        gq = {}

        def q_adds(c):
            gq[c] = work.tile([P, 2048], BF16, tag="gq", name="gq%d" % c, align_bytes=64)
            for w in range(2):
                add_rel(gq[c][:, w * 1024 : (w + 1) * 1024], xq[c], w)

        def q_quant(c):
            quant(qc[:, c * 512 : (c + 1) * 512], qs[:, c * 512 : (c + 1) * 512], gq[c][:])

        sc = {}
        st = {}
        e_t = {}
        t_t = {}
        pt = {}
        gp = {}
        pq = {}
        o_ps = {}

        def scores(i, w):
            off = ((i // 2) * 2 + w) * 256 + (i % 2) * P
            tiles = []
            for h in range(2):
                t = bank(2 * w + h, "sc%d_%d_%d" % (i, w, h))
                nc.tensor.matmul_mx(
                    out=t[:],
                    lhsT=qc[:, off : off + P].bitcast(FP8X4),
                    lhsT_scale=qs[:, off : off + P],
                    rhs=kc[w][:, h * 512 : (h + 1) * 512].bitcast(FP8X4),
                    rhs_scale=ks[w][:, h * 512 : (h + 1) * 512],
                    start=True,
                    stop=True,
                )
                tiles.append(t)
            sc[(i, w)] = tiles

        def red(i, w, h):
            if (w, h) == (0, 0):
                st[i] = {
                    "mx": small.tile([P, 4], F32, tag="mx", name="mx%d" % i),
                    "nb": small.tile([P, 2], F32, tag="nb", name="nb%d" % i),
                    "sm": small.tile([P, 4], F32, tag="sm", name="sm%d" % i),
                    "tot": small.tile([P, 2], F32, tag="tot", name="tot%d" % i),
                    "rc": small.tile([P, 2], F32, tag="rc", name="rc%d" % i),
                }
            nc.vector.tensor_reduce(
                out=st[i]["mx"][:, 2 * w + h : 2 * w + h + 1], in_=sc[(i, w)][h][:], axis=AX.X, op=ALU.max
            )

        def nbias(i, w):
            mx = st[i]["mx"]
            nc.vector.tensor_scalar(
                out=st[i]["nb"][:, w : w + 1],
                in0=mx[:, 2 * w : 2 * w + 1],
                scalar1=mx[:, 2 * w + 1 : 2 * w + 2],
                scalar2=-scale,
                op0=ALU.max,
                op1=ALU.mult,
            )

        def exps(i, w):
            e = work.tile([P, L], F32, tag="e%d" % w, name="e%d_%d" % (i, w))
            for h in range(2):
                nc.scalar.activation(
                    out=e[:, h * 512 : (h + 1) * 512],
                    in_=sc[(i, w)][h][:],
                    func=ACT.Exp,
                    bias=st[i]["nb"][:, w : w + 1],
                    scale=scale,
                    accum_out=st[i]["sm"][:, 2 * w + h : 2 * w + h + 1],
                )
            e_t[(i, w)] = e

        def total(i):
            nc.vector.tensor_reduce(
                out=st[i]["tot"][:],
                in_=st[i]["sm"][:].rearrange("p (w h) -> p w h", h=2),
                axis=AX.X,
                op=ALU.add,
            )

        def recip(i):
            nc.vector.reciprocal(out=st[i]["rc"][:], in_=st[i]["tot"][:])

        def new_t(i, w):
            t_t[(i, w)] = work.tile([P, L], F32, tag="t%d" % w, name="t%d_%d" % (i, w))

        def pool_mul(i, lo, hi):
            new_t(i, 1)
            for b in range(lo, hi, 2):
                nc.gpsimd.tensor_tensor(
                    out=t_t[(i, 1)][:, b * P : (b + 2) * P],
                    in0=e_t[(i, 1)][:, b * P : (b + 2) * P],
                    in1=m_sb[1][:, i * L + b * P : i * L + (b + 2) * P],
                    op=ALU.mult,
                )

        def pool_scale(i, lo, hi):
            nc.gpsimd.tensor_scalar(
                out=t_t[(i, 1)][:, lo * P : hi * P],
                in0=t_t[(i, 1)][:, lo * P : hi * P],
                scalar1=st[i]["rc"][:, 1:2],
                scalar2=0.0,
                op0=ALU.mult,
                op1=ALU.add,
            )

        def masked(i, w, lo, hi):
            if (i, w) not in t_t:
                new_t(i, w)
            nc.vector.scalar_tensor_tensor(
                out=t_t[(i, w)][:, lo * P : hi * P],
                in0=e_t[(i, w)][:, lo * P : hi * P],
                scalar=st[i]["rc"][:, w : w + 1],
                in1=m_sb[w][:, i * L + lo * P : i * L + hi * P],
                op0=ALU.mult,
                op1=ALU.mult,
            )

        def flip(i, g):
            x = bank(4 + g, "pt%d_%d" % (i, g))
            for t in range(4):
                kb = 4 * g + t
                for w in range(2):
                    nc.tensor.matmul(
                        out=x[:, t * P : (t + 1) * P],
                        lhsT=t_t[(i, w)][:, kb * P : (kb + 1) * P],
                        rhs=ident[:],
                        is_transpose=True,
                        start=(w == 0),
                        stop=(w == 1),
                    )
            pt[(i, g)] = x

        def round_p(i, g, on_vector=False):
            if g == 0:
                gp[i] = work.tile([P, L], BF16, tag="gp", name="gp%d" % i, align_bytes=64)
            dst = gp[i][:, g * 512 : (g + 1) * 512].rearrange("p (r t) -> p r t", t=4)
            src = pt[(i, g)][:].rearrange("p (t r) -> p r t", t=4)
            if on_vector:
                nc.vector.tensor_copy(out=dst, in_=src)
            else:
                nc.scalar.copy(out=dst, in_=src)

        def quant_p(i, lo, hi):
            if lo == 0:
                pq[i] = (
                    work.tile([P, 256], U32, tag="pc", name="pc%d" % i, align_bytes=64),
                    work.tile([P, 256], U8, tag="ps", name="ps%d" % i, align_bytes=64),
                )
            codes, scales = pq[i]
            quant(codes[:, lo * P : hi * P], scales[:, lo * P : hi * P], gp[i][:, lo * 512 : hi * 512])

        def pv(i, g):
            codes, scales = pq[i]
            if g == 0:
                o_ps[i] = bank(6 + i % 2, "o%d" % i)
            nc.tensor.matmul_mx(
                out=o_ps[i][:],
                lhsT=codes[:, g * P : (g + 1) * P].bitcast(FP8X4),
                lhsT_scale=scales[:, g * P : (g + 1) * P],
                rhs=vc[:, g * D : (g + 1) * D].bitcast(FP8X4),
                rhs_scale=vs[:, g * D : (g + 1) * D],
                start=(g == 0),
                stop=(g == 1),
            )

        def store(i):
            o = work.tile([P, D], F32, tag="o_sb", name="o_sb%d" % i, bufs=3)
            nc.scalar.copy(out=o[:], in_=o_ps[i][:])
            nc.sync.dma_start(out=out2[i * P : (i + 1) * P, :], in_=o[:])

        for c in range(4):
            for w in range(2):
                add_rel(gk[w][c // 2][:, (c % 2) * 1024 : (c % 2 + 1) * 1024], xk[c], w)
                if c == 2:
                    quant_k(w, 0)
        q_adds(0)
        quant_k(0, 1)
        quant_k(1, 1)
        q_quant(0)
        scores(0, 0)
        scores(0, 1)
        q_adds(1)

        for j in range(NT):
            red(j, 0, 0)
            if j >= 1:
                total(j - 1)
            red(j, 0, 1)
            if j >= 1:
                recip(j - 1)
                pool_scale(j - 1, VB, 8)
            red(j, 1, 0)
            nbias(j, 0)
            exps(j, 0)
            if j + 1 < NT:
                scores(j + 1, 0)
            red(j, 1, 1)
            if j == 0:
                quant_v(0)
            if j >= 3:
                quant_p(j - 3, 0, 2)
                pv(j - 3, 0)
                pv(j - 3, 1)
            nbias(j, 1)
            exps(j, 1)
            if j + 1 < NT:
                pool_mul(j, VB, 8)
                scores(j + 1, 1)
            if j in (1, 2):
                q_adds(j + 1)
            if j >= 1:
                masked(j - 1, 0, 0, 8)
                masked(j - 1, 1, 0, VB)
            if j >= 2:
                round_p(j - 2, 0)
                round_p(j - 2, 1)
            if j >= 1:
                flip(j - 1, 0)
                flip(j - 1, 1)
            if j >= 3:
                store(j - 3)
            if j == 0:
                q_quant(1)
                quant_v(1)
            if j in (1, 2):
                q_quant(j + 1)

        z = NT - 1
        total(z)
        quant_p(z - 2, 0, 2)
        pv(z - 2, 0)
        pv(z - 2, 1)
        recip(z)
        round_p(z - 1, 0)
        round_p(z - 1, 1)
        masked(z, 0, 0, 4)
        masked(z, 1, 0, 4)
        flip(z, 0)
        masked(z, 0, 4, 8)
        masked(z, 1, 4, 8)
        flip(z, 1)
        store(z - 2)
        quant_p(z - 1, 0, 2)
        pv(z - 1, 0)
        pv(z - 1, 1)
        round_p(z, 0)
        quant_p(z, 0, 1)
        pv(z, 0)
        round_p(z, 1, on_vector=True)
        store(z - 1)
        quant_p(z, 1, 2)
        pv(z, 1)
        store(z)
